import numpy as np
import ml_dtypes


def mxq(x, axis, fmt="e4m3"):
    dtype, down = {"e4m3": (ml_dtypes.float8_e4m3fn, 7), "e5m2": (ml_dtypes.float8_e5m2, 14)}[fmt]
    v = np.moveaxis(np.asarray(x, np.float32).astype(ml_dtypes.bfloat16).astype(np.float64), axis, -1)
    blocks = v.reshape(v.shape[:-1] + (-1, 32))
    amax = np.abs(blocks).max(-1, keepdims=True)
    byte = np.maximum(np.where(amax > 0, np.frexp(amax)[1] - 1 + 127, 0) - down, 1)
    scale = np.exp2(byte - 127.0)
    codes = (blocks / scale).astype(np.float32).astype(dtype).astype(np.float64)
    return np.moveaxis((codes * scale).reshape(v.shape), -1, axis)


WIDE = False


def mx_kscale(k):
    if not WIDE:
        return np.ones(k)
    levels = np.array([10, -10, 5, -5, 0])
    if k % 512:
        return np.exp2(np.random.permutation(np.resize(levels, k // 32))).repeat(32)
    a = np.empty((k // 512, 16))
    for p in range(k // 512):
        a[p, :8] = np.random.permutation(np.resize(levels, 8))
        for g in range(8):
            far = levels[np.abs(levels - a[p, g]) >= 10]
            a[p, g + 8] = far[np.random.randint(len(far))]
    return np.exp2(a.ravel()).repeat(32)


BF16 = ml_dtypes.bfloat16


def bf(x):
    return np.asarray(x, np.float32).astype(BF16)


def f64(x):
    return np.asarray(x).astype(np.float64)


B, D, H = 256, 1024, 2048
M_SCALE = 1.5


def draw0():
    s, t = mx_kscale(D), mx_kscale(H)
    return {'x': bf(np.random.standard_normal((B, D)) * s),
            'h_prev': bf(np.random.standard_normal((B, H)) * t),
            'c_prev': bf(np.random.standard_normal((B, H))),
            'W_ih': bf(np.random.standard_normal((2 * H, D)) * 0.7 / np.sqrt(D) / s[None, :]),
            'b_ih': bf(np.random.standard_normal(2 * H) * 0.2),
            'W_hh': bf(np.random.standard_normal((2 * H, H)) * 0.7 / np.sqrt(H) / t[None, :]),
            'b_hh': bf(np.random.standard_normal(2 * H) * 0.2),
            'log_lambda': bf(np.log(np.random.uniform(0.05, 0.5, H))),
            'z_bias': bf(np.random.standard_normal(H) * 0.2),
            'm_bias': bf(np.random.standard_normal(H) * 0.2)}


def core(x, h_prev, c_prev, W_ih, b_ih, W_hh, b_hh, log_lambda, z_bias, m_bias):
    gates = ((mxq(f64(x), 1, 'e4m3') @ mxq(f64(W_ih), 1, 'e4m3').T) + f64(b_ih)
             + (mxq(f64(h_prev), 1, 'e4m3') @ mxq(f64(W_hh), 1, 'e4m3').T) + f64(b_hh))
    z_raw, m_raw = gates[:, :H], gates[:, H:]
    z_t = np.tanh(z_raw + f64(z_bias))
    M_t = M_SCALE * np.tanh(m_raw + f64(m_bias))
    A_base = -np.exp(f64(log_lambda))
    innov = z_t - M_t * (A_base * f64(c_prev))
    return z_t, M_t, innov


def e4m3fn_bytes(y):
    return np.clip(np.asarray(y, np.float64), -448.0, 448.0).astype(np.float32).astype(ml_dtypes.float8_e4m3fn).view(np.uint8)


def e4m3fn_values(b):
    return np.asarray(b, np.uint8).view(ml_dtypes.float8_e4m3fn).astype(np.float64)


def setup_inputs():
    d = draw0()
    x0 = np.asarray(d['W_hh']).astype(np.float64)
    s = (np.max(np.abs(x0), axis=(0,), keepdims=True) / 448.0).astype(np.float32)
    out = {}
    for k, v in d.items():
        if k == 'W_hh':
            out['W_hh_bytes'] = e4m3fn_bytes(x0 / s.astype(np.float64))
            out['W_hh_scale'] = s
        else:
            out[k] = v
    return out


def reference(x, h_prev, c_prev, W_ih, b_ih, W_hh_bytes, W_hh_scale, b_hh, log_lambda, z_bias, m_bias):
    return core(x, h_prev, c_prev, W_ih, b_ih, e4m3fn_values(W_hh_bytes) * W_hh_scale.astype(np.float64), b_hh, log_lambda, z_bias, m_bias)

@@ -1,0 +1,321 @@
+from contextlib import ExitStack
+
+import concourse.mybir as mybir
+from concourse.masks import make_identity
+
+B, D, H = 256, 1024, 2048
+FLOPS = 2 * B * (2 * H) * (D + H)
+
+F32 = mybir.dt.float32
+BF16 = mybir.dt.bfloat16
+U32 = mybir.dt.uint32
+U8 = mybir.dt.uint8
+FP8 = mybir.dt.float8_e4m3fn
+FP8X4 = mybir.dt.float8_e4m3fn_x4
+ACT = mybir.ActivationFunctionType
+ALU = mybir.AluOpType
+
+P = 128
+NU = H // P
+GX = D // 512
+GH = H // 512
+M_SCALE = 1.5
+Z, M = 0, 1
+CT_FIRST = 1
+
+
+def tile_koslmcell_pa_kernel(
+    tc, x, h_prev, c_prev, W_ih, b_ih, W_hh_bytes, W_hh_scale, b_hh, log_lambda, z_bias, m_bias, out_0, out_1, out_2
+):
+    nc = tc.nc
+    with ExitStack() as ctx:
+        const = ctx.enter_context(tc.tile_pool(name="const", bufs=1))
+        loads = ctx.enter_context(tc.tile_pool(name="loads", bufs=4))
+        work = ctx.enter_context(tc.tile_pool(name="work", bufs=3))
+        stage = ctx.enter_context(tc.tile_pool(name="stage", bufs=3))
+        tp = ctx.enter_context(tc.psum_pool(name="tp", bufs=4))
+        accp = ctx.enter_context(tc.psum_pool(name="accp", bufs=1))
+        otp = ctx.enter_context(tc.psum_pool(name="otp", bufs=1))
+        ctx.enter_context(tc.manual_schedule())
+
+        whb_view = W_hh_bytes.rearrange("(s j p) k -> j p s k", s=2, p=P)
+        wih_view = W_ih.rearrange("(s j p) k -> j p s k", s=2, p=P)
+        out_views = [o.rearrange("(bh p) n -> p bh n", p=P) for o in (out_0, out_1, out_2)]
+        scale_row = W_hh_scale.rearrange("o k -> (o k)")
+
+        whb, wih, wb, gh, gi = {}, {}, {}, {}, {}
+        ch, sh, ci, si, acc = {}, {}, {}, {}, {}
+        zT, tT, prodT, st = {}, {}, {}, {}
+
+        ident_f = const.tile([P, P], F32, name="ident_f")
+        make_identity(nc, ident_f[:])
+        ident_b = const.tile([P, P], BF16, name="ident_b")
+        make_identity(nc, ident_b[:])
+        warm = const.tile([P, 1], F32, name="warm")
+        nc.vector.memset(warm[:], 0.0)
+        warm2 = const.tile([P, 1], F32, name="warm2")
+        nc.scalar.activation(out=warm2[:], in_=warm[:], func=ACT.Tanh)
+        vrows = const.tile([P, P], BF16, name="vrows")
+        nc.vector.memset(vrows[:], 0.0)
+
+        def load_whb(i):
+            whb[i] = loads.tile([P, 2, H], U8, name="whb", tag="whb")
+            nc.sync.dma_start(out=whb[i][:], in_=whb_view[i])
+
+        def load_wih(i):
+            wih[i] = loads.tile([P, 2, D], BF16, name="wih", tag="wih")
+            nc.sync.dma_start(out=wih[i][:], in_=wih_view[i])
+
+        sbc = const.tile([P, 2, H], F32, name="sbc")
+        whb[0] = loads.tile([P, 2, H], U8, name="whb", tag="whb")
+        nc.sync.dma_start(out=sbc[:, 0, 0:512], in_=scale_row[0:512].partition_broadcast(P))
+        nc.sync.dma_start(out=whb[0][:, M, :], in_=whb_view[0][:, M, :])
+        for c in range(1, 4):
+            nc.sync.dma_start(
+                out=sbc[:, 0, c * 512 : (c + 1) * 512], in_=scale_row[c * 512 : (c + 1) * 512].partition_broadcast(P)
+            )
+        nc.sync.dma_start(out=whb[0][:, Z, :], in_=whb_view[0][:, Z, :])
+        for c in range(4):
+            nc.scalar.copy(out=sbc[:, 1, c * 512 : (c + 1) * 512], in_=sbc[:, 0, c * 512 : (c + 1) * 512])
+        load_whb(1)
+        x_sb = const.tile([P, 2, D], BF16, name="x_sb")
+        nc.sync.dma_start(out=x_sb[:], in_=x.rearrange("(bt p) k -> p bt k", p=P))
+        h_sb = const.tile([P, 2, H], BF16, name="h_sb")
+        nc.sync.dma_start(out=h_sb[:], in_=h_prev.rearrange("(bt p) k -> p bt k", p=P))
+        load_whb(2)
+        load_wih(0)
+        nc.sync.dma_start(out=vrows[0:32, :], in_=b_ih.rearrange("(j p) -> j p", p=P))
+        nc.sync.dma_start(out=vrows[32:64, :], in_=b_hh.rearrange("(j p) -> j p", p=P))
+        nc.sync.dma_start(out=vrows[64:80, :], in_=z_bias.rearrange("(j p) -> j p", p=P))
+        nc.sync.dma_start(out=vrows[80:96, :], in_=m_bias.rearrange("(j p) -> j p", p=P))
+        nc.sync.dma_start(out=vrows[96:112, :], in_=log_lambda.rearrange("(j p) -> j p", p=P))
+        load_wih(1)
+        c_sb = const.tile([P, 2, H], BF16, name="c_sb")
+        nc.sync.dma_start(out=c_sb[:], in_=c_prev.rearrange("(bh p) n -> p bh n", p=P))
+        load_whb(3)
+        load_wih(2)
+        load_wih(3)
+
+        def turn(words, g0, dst):
+            bank = tp.tile([P, 2, 2, P], F32, name="bank", tag="tp")
+            for gg in range(2):
+                for u in range(2):
+                    g = g0 + gg
+                    nc.tensor.transpose(bank[:, gg, u, :], words[:, 256 * g + u : 256 * (g + 1) : 2], ident_f[:])
+            nc.scalar.copy(out=dst, in_=bank[:].rearrange("p g u r -> p g r u"))
+
+        def widen(i, pieces):
+            if i not in wb:
+                wb[i] = work.tile([P, 2 * H], BF16, name="wb", tag="wb")
+            src = whb[i][:].rearrange("p s k -> p (s k)").bitcast(FP8)
+            scl = sbc[:].rearrange("p s k -> p (s k)")
+            for a, b, sa in pieces:
+                nc.vector.tensor_tensor(out=wb[i][:, a:b], in0=src[:, a:b], in1=scl[:, sa : sa + b - a], op=ALU.mult)
+
+        def turn_ih(i):
+            gi[i] = work.tile([P, 2 * GX * 512], BF16, name="gi", tag="gi", align_bytes=64)
+            for s in (M, Z):
+                dst = gi[i][:, s * 1024 : (s + 1) * 1024].bitcast(F32).rearrange("p (g r u) -> p g r u", g=2, u=2)
+                turn(wih[i][:, s, :].bitcast(F32), 0, dst)
+
+        def turn_hh(i, s):
+            if s == M:
+                gh[i] = work.tile([P, 2 * GH * 512], BF16, name="gh", tag="gh", align_bytes=64)
+            for g0 in (0, 2):
+                o = s * 2048 + g0 * 512
+                dst = gh[i][:, o : o + 1024].bitcast(F32).rearrange("p (g r u) -> p g r u", g=2, u=2)
+                turn(wb[i][:, s * H : (s + 1) * H].bitcast(F32), g0, dst)
+
+        def quantize_ih(i):
+            ci[i] = work.tile([P, 2 * GX * P], U32, name="ci", tag="ci", align_bytes=64)
+            si[i] = work.tile([P, 2 * GX * P], U8, name="si", tag="si", align_bytes=64)
+            nc.vector.quantize_mx(out=ci[i][:].bitcast(FP8X4), scales=si[i][:], in_=gi[i][:])
+
+        def quantize_hh(i, split):
+            ch[i] = work.tile([P, 2 * GH * P], U32, name="ch", tag="ch", align_bytes=64)
+            sh[i] = work.tile([P, 2 * GH * P], U8, name="sh", tag="sh", align_bytes=64)
+            if split:
+                for s in (M, Z):
+                    cols = slice(s * GH * P, (s + 1) * GH * P)
+                    nc.vector.quantize_mx(
+                        out=ch[i][:, cols].bitcast(FP8X4), scales=sh[i][:, cols], in_=gh[i][:, s * 2048 : (s + 1) * 2048]
+                    )
+            else:
+                nc.vector.quantize_mx(out=ch[i][:].bitcast(FP8X4), scales=sh[i][:], in_=gh[i][:])
+
+        def multiply(i, s, which):
+            if which == "x":
+                acc[i, s] = accp.tile([P, B], F32, name="acc%d" % s, tag="acc%d" % s)
+                wc, ws, ac, as_, n = ci[i], si[i], xq, xs, GX
+            else:
+                wc, ws, ac, as_, n = ch[i], sh[i], hq, hs, GH
+            for g in range(n):
+                wcol = s * n + g
+                nc.tensor.matmul_mx(
+                    out=acc[i, s][:],
+                    lhsT=wc[:, wcol * P : (wcol + 1) * P].bitcast(FP8X4),
+                    lhsT_scale=ws[:, wcol * P : (wcol + 1) * P],
+                    rhs=ac[:, g * B : (g + 1) * B].bitcast(FP8X4),
+                    rhs_scale=as_[:, g * B : (g + 1) * B],
+                    start=(which == "x" and g == 0),
+                    stop=(which == "h" and g == n - 1),
+                )
+
+        def tanh_m(i):
+            tT[i] = work.tile([P, B], F32, name="tT", tag="tT")
+            nc.scalar.activation(out=tT[i][:], in_=acc[i, M][:], func=ACT.Tanh, bias=bias[:, NU + i : NU + i + 1])
+
+        def tanh_z(i):
+            zT[i] = work.tile([P, B], F32, name="zT", tag="zT")
+            nc.scalar.activation(out=zT[i][:], in_=acc[i, Z][:], func=ACT.Tanh, bias=bias[:, i : i + 1])
+
+        def product(i):
+            prodT[i] = work.tile([P, B], F32, name="prodT", tag="prodT")
+            nc.vector.scalar_tensor_tensor(
+                out=prodT[i][:], in0=tT[i][:], scalar=lam15[:, i : i + 1], in1=cT[:, i, :], op0=ALU.mult, op1=ALU.mult
+            )
+
+        def store(i, k):
+            if i >= NU - 2:
+                nc.scalar.dma_start(out=out_views[k][:, :, i * P : (i + 1) * P], in_=st[k][:])
+            elif i % 2 == 1:
+                nc.scalar.dma_start(out=out_views[k][:, :, (i - 1) * P : (i + 1) * P], in_=st[k][:])
+
+        def outputs(i):
+            alone = i >= NU - 2
+            half = 0 if alone else i % 2
+            if half == 0:
+                for k in range(3):
+                    st[k] = stage.tile([P, 2, P if alone else 2 * P], F32, name="st%d" % k, tag="st%d" % k)
+            cols = slice(half * P, (half + 1) * P)
+            ot_a = otp.tile([P, 4, P], F32, name="ot_a", tag="ot_a")
+            for bh in range(2):
+                nc.tensor.transpose(ot_a[:, bh, :], zT[i][:, bh * P : (bh + 1) * P], ident_f[:])
+            for bh in range(2):
+                nc.tensor.transpose(ot_a[:, 2 + bh, :], tT[i][:, bh * P : (bh + 1) * P], ident_f[:])
+            nc.scalar.copy(out=st[0][:, :, cols], in_=ot_a[:, 0:2, :])
+            nc.scalar.activation(out=st[1][:, :, cols], in_=ot_a[:, 2:4, :], func=ACT.Copy, scale=M_SCALE)
+            for k in range(2):
+                store(i, k)
+            ot_b = otp.tile([P, 2, P], F32, name="ot_b", tag="ot_b")
+            for bh in range(2):
+                rows = slice(bh * P, (bh + 1) * P)
+                nc.tensor.matmul(
+                    out=ot_b[:, bh, :], lhsT=zT[i][:, rows], rhs=ident_f[:], is_transpose=True, start=True, stop=False
+                )
+                nc.tensor.matmul(
+                    out=ot_b[:, bh, :], lhsT=prodT[i][:, rows], rhs=ident_f[:], is_transpose=True, start=False, stop=True
+                )
+            nc.scalar.copy(out=st[2][:, :, cols], in_=ot_b[:])
+            store(i, 2)
+
+        widen(0, [(H + c * 512, H + (c + 1) * 512, c * 512) for c in range(4)] + [(0, H, 0)])
+        turn_hh(0, M)
+        turn_hh(0, Z)
+        widen(1, [(H, 2 * H, 0), (0, H, 0)])
+        widen(2, [(H, 2 * H, 0)])
+
+        gx = const.tile([P, GX * B * 4], BF16, name="gx", align_bytes=64)
+        gxw = gx[:].bitcast(F32).rearrange("p (g b u) -> p g b u", g=GX, u=2)
+        for bt in range(2):
+            turn(x_sb[:, bt, :].bitcast(F32), 0, gxw[:, :, bt * P : (bt + 1) * P, :])
+        ga = const.tile([P, GH * B * 4], BF16, name="ga", align_bytes=64)
+        gaw = ga[:].bitcast(F32).rearrange("p (g b u) -> p g b u", g=GH, u=2)
+        for bt in range(2):
+            for g0 in (0, 2):
+                turn(h_sb[:, bt, :].bitcast(F32), g0, gaw[:, g0 : g0 + 2, bt * P : (bt + 1) * P, :])
+        xq = const.tile([P, GX * B], U32, name="xq", align_bytes=64)
+        xs = const.tile([P, GX * B], U8, name="xs", align_bytes=64)
+        nc.vector.quantize_mx(out=xq[:].bitcast(FP8X4), scales=xs[:], in_=gx[:])
+        hq = const.tile([P, GH * B], U32, name="hq", align_bytes=64)
+        hs = const.tile([P, GH * B], U8, name="hs", align_bytes=64)
+        nc.vector.quantize_mx(out=hq[:].bitcast(FP8X4), scales=hs[:], in_=ga[:])
+
+        turn_ih(0)
+        vps = tp.tile([P, P], BF16, name="vps", tag="tp")
+        nc.tensor.transpose(vps[:], vrows[:], ident_b[:])
+        vT = const.tile([P, P], F32, name="vT")
+        nc.scalar.copy(out=vT[:], in_=vps[:])
+        lam = const.tile([P, NU], F32, name="lam")
+        nc.scalar.activation(out=lam[:], in_=vT[:, 96:112], func=ACT.Exp)
+        bias0 = const.tile([P, 2 * NU], F32, name="bias0")
+        nc.vector.tensor_tensor(out=bias0[:], in0=vT[:, 0:32], in1=vT[:, 32:64], op=ALU.add)
+        lam15 = const.tile([P, NU], F32, name="lam15")
+        nc.vector.tensor_scalar(out=lam15[:], in0=lam[:], scalar1=M_SCALE, scalar2=None, op0=ALU.mult)
+        bias = const.tile([P, 2 * NU], F32, name="bias")
+        nc.vector.tensor_tensor(out=bias[:], in0=bias0[:], in1=vT[:, 64:96], op=ALU.add)
+
+        turn_hh(1, M)
+        turn_hh(1, Z)
+        load_whb(4)
+        load_wih(4)
+
+        cT = const.tile([P, NU, B], BF16, name="cT")
+
+        def turn_c(first, count):
+            for jj in range(first, first + count):
+                cps = tp.tile([P, 2, 2, P], BF16, name="cps", tag="tp")
+                for j2 in range(2):
+                    for bh in range(2):
+                        j = 2 * jj + j2
+                        nc.tensor.transpose(cps[:, j2, bh, :], c_sb[:, bh, j * P : (j + 1) * P], ident_b[:])
+                nc.scalar.copy(out=cT[:, 2 * jj : 2 * jj + 2, :], in_=cps[:].rearrange("p j bh b -> p j (bh b)"))
+
+        turn_ih(1)
+        last = NU - 1
+        for i in range(1, last):
+            if i == 2:
+                turn_hh(i, M)
+                widen(i, [(0, H, 0)])
+                turn_hh(i, Z)
+            elif i > 2:
+                widen(i, [(0, 2 * H, 0)])
+                turn_hh(i, M)
+                turn_hh(i, Z)
+            if 1 < i and i + 3 < NU:
+                load_whb(i + 3)
+                load_wih(i + 3)
+            quantize_ih(i - 1)
+            quantize_hh(i - 1, False)
+            if i >= 2:
+                product(i - 2)
+            if i == 1:
+                turn_c(0, CT_FIRST)
+            multiply(i - 1, M, "x")
+            multiply(i - 1, M, "h")
+            tanh_m(i - 1)
+            turn_ih(i + 1)
+            multiply(i - 1, Z, "x")
+            multiply(i - 1, Z, "h")
+            tanh_z(i - 1)
+            if i == 1:
+                turn_c(CT_FIRST, NU // 2 - CT_FIRST)
+            if i >= 2:
+                outputs(i - 2)
+
+        widen(last, [(H, 2 * H, 0)])
+        turn_hh(last, M)
+        quantize_ih(last - 1)
+        quantize_hh(last - 1, False)
+        product(last - 2)
+        multiply(last - 1, M, "x")
+        multiply(last - 1, M, "h")
+        tanh_m(last - 1)
+        multiply(last - 1, Z, "x")
+        multiply(last - 1, Z, "h")
+        tanh_z(last - 1)
+        widen(last, [(0, H, 0)])
+        turn_hh(last, Z)
+        outputs(last - 2)
+        quantize_ih(last)
+        quantize_hh(last, True)
+        product(last - 1)
+        multiply(last, M, "x")
+        multiply(last, Z, "x")
+        multiply(last, M, "h")
+        tanh_m(last)
+        multiply(last, Z, "h")
+        tanh_z(last)
+        outputs(last - 1)
+        product(last)
+        outputs(last)

@@ -1,3 +1,4 @@
+import math
 from contextlib import ExitStack
 
 import concourse.mybir as mybir
@@ -22,6 +23,11 @@ GH = H // 512
 M_SCALE = 1.5
 Z, M = 0, 1
 CT_FIRST = 1
+N_OFF = 0
+LW = NU - 1 - N_OFF
+OFF = list(range(LW + 1, NU))
+DIRECT = False
+ALONE = (NU - 2, NU - 1)
 
 
 def tile_koslmcell_pa_kernel(
@@ -33,6 +39,7 @@ def tile_koslmcell_pa_kernel(
         loads = ctx.enter_context(tc.tile_pool(name="loads", bufs=4))
         work = ctx.enter_context(tc.tile_pool(name="work", bufs=3))
         stage = ctx.enter_context(tc.tile_pool(name="stage", bufs=3))
+        offp = ctx.enter_context(tc.tile_pool(name="offp", bufs=2))
         tp = ctx.enter_context(tc.psum_pool(name="tp", bufs=4))
         accp = ctx.enter_context(tc.psum_pool(name="accp", bufs=1))
         otp = ctx.enter_context(tc.psum_pool(name="otp", bufs=1))
@@ -46,6 +53,8 @@ def tile_koslmcell_pa_kernel(
         whb, wih, wb, gh, gi = {}, {}, {}, {}, {}
         ch, sh, ci, si, acc = {}, {}, {}, {}, {}
         zT, tT, prodT, st = {}, {}, {}, {}
+        whbo, wbo, obank, pl = {}, {}, {}, {}
+        ot, ott, ob, started = {}, {}, {}, set()
 
         ident_f = const.tile([P, P], F32, name="ident_f")
         make_identity(nc, ident_f[:])
@@ -68,8 +77,9 @@ def tile_koslmcell_pa_kernel(
 
         sbc = const.tile([P, 2, H], F32, name="sbc")
         whb[0] = loads.tile([P, 2, H], U8, name="whb", tag="whb")
+        nc.sync.dma_start(out=whb[0][:, M, 0:512], in_=whb_view[0][:, M, 0:512])
         nc.sync.dma_start(out=sbc[:, 0, 0:512], in_=scale_row[0:512].partition_broadcast(P))
-        nc.sync.dma_start(out=whb[0][:, M, :], in_=whb_view[0][:, M, :])
+        nc.sync.dma_start(out=whb[0][:, M, 512:H], in_=whb_view[0][:, M, 512:H])
         for c in range(1, 4):
             nc.sync.dma_start(
                 out=sbc[:, 0, c * 512 : (c + 1) * 512], in_=scale_row[c * 512 : (c + 1) * 512].partition_broadcast(P)
@@ -89,20 +99,27 @@ def tile_koslmcell_pa_kernel(
         nc.sync.dma_start(out=vrows[64:80, :], in_=z_bias.rearrange("(j p) -> j p", p=P))
         nc.sync.dma_start(out=vrows[80:96, :], in_=m_bias.rearrange("(j p) -> j p", p=P))
         nc.sync.dma_start(out=vrows[96:112, :], in_=log_lambda.rearrange("(j p) -> j p", p=P))
+        if OFF:
+            sT = const.tile([P, GH, 4], F32, name="sT")
+            nc.sync.dma_start(out=sT[:], in_=W_hh_scale.rearrange("o (g p t) -> p (o g) t", p=P, t=4))
         load_wih(1)
         c_sb = const.tile([P, 2, H], BF16, name="c_sb")
         nc.sync.dma_start(out=c_sb[:], in_=c_prev.rearrange("(bh p) n -> p bh n", p=P))
         load_whb(3)
         load_wih(2)
         load_wih(3)
+        for j in OFF:
+            whbo[j] = const.tile([P, 2, H], U8, name="whbo%d" % j)
+            nc.sync.dma_start(out=whbo[j][:], in_=whb_view[j])
+            gh[j] = const.tile([P, 2 * GH * 512], BF16, name="gho%d" % j, align_bytes=64)
 
-        def turn(words, g0, dst):
+        def turn(words, g0, dst, n=2):
             bank = tp.tile([P, 2, 2, P], F32, name="bank", tag="tp")
-            for gg in range(2):
+            for gg in range(n):
                 for u in range(2):
                     g = g0 + gg
                     nc.tensor.transpose(bank[:, gg, u, :], words[:, 256 * g + u : 256 * (g + 1) : 2], ident_f[:])
-            nc.scalar.copy(out=dst, in_=bank[:].rearrange("p g u r -> p g r u"))
+            nc.scalar.copy(out=dst, in_=bank[:, 0:n].rearrange("p g u r -> p g r u"))
 
         def widen(i, pieces):
             if i not in wb:
@@ -118,13 +135,45 @@ def tile_koslmcell_pa_kernel(
                 dst = gi[i][:, s * 1024 : (s + 1) * 1024].bitcast(F32).rearrange("p (g r u) -> p g r u", g=2, u=2)
                 turn(wih[i][:, s, :].bitcast(F32), 0, dst)
 
-        def turn_hh(i, s):
-            if s == M:
+        def turn_hh(i, s, runs=((0, 2), (2, 2))):
+            if i not in gh:
                 gh[i] = work.tile([P, 2 * GH * 512], BF16, name="gh", tag="gh", align_bytes=64)
-            for g0 in (0, 2):
+            for g0, n in runs:
                 o = s * 2048 + g0 * 512
-                dst = gh[i][:, o : o + 1024].bitcast(F32).rearrange("p (g r u) -> p g r u", g=2, u=2)
-                turn(wb[i][:, s * H : (s + 1) * H].bitcast(F32), g0, dst)
+                dst = gh[i][:, o : o + 512 * n].bitcast(F32).rearrange("p (g r u) -> p g r u", g=n, u=2)
+                turn(wb[i][:, s * H : (s + 1) * H].bitcast(F32), g0, dst, n)
+
+        def off_cast(j, g):
+            wbo[j, g] = offp.tile([P, 2, 512], BF16, name="wbo", tag="wbo")
+            for s in (M, Z):
+                nc.scalar.copy(out=wbo[j, g][:, s, :], in_=whbo[j][:, s, g * 512 : (g + 1) * 512].bitcast(FP8))
+
+        def off_turn(j, g):
+            obank[j, g] = tp.tile([P, 2, 2, P], F32, name="bank", tag="tp")
+            for s in (M, Z):
+                words = wbo[j, g][:, s, :].bitcast(F32)
+                for u in range(2):
+                    nc.tensor.transpose(obank[j, g][:, s, u, :], words[:, u : 256 : 2], ident_f[:])
+
+        def off_scale(j, g):
+            bv = obank[j, g][:].bitcast(BF16).rearrange("p s u (r e) -> p s u r e", e=2)
+            dst = gh[j][:].rearrange("p (s g r t) -> p s g r t", s=2, g=GH, t=4)
+            if not DIRECT:
+                pl[j, g] = offp.tile([P, 4, 2, P], BF16, name="pl", tag="pl")
+            for u in range(2):
+                for e in range(2):
+                    t = 2 * u + e
+                    nc.scalar.activation(
+                        out=dst[:, :, g, :, t] if DIRECT else pl[j, g][:, t, :, :],
+                        in_=bv[:, :, u, :, e],
+                        func=ACT.Copy,
+                        scale=sT[:, g, t : t + 1],
+                    )
+
+        def off_weave(j, g):
+            if not DIRECT:
+                dst = gh[j][:].rearrange("p (s g r t) -> p s g r t", s=2, g=GH, t=4)
+                nc.scalar.copy(out=dst[:, :, g, :, :], in_=pl[j, g][:].rearrange("p t s r -> p s r t"))
 
         def quantize_ih(i):
             ci[i] = work.tile([P, 2 * GX * P], U32, name="ci", tag="ci", align_bytes=64)
@@ -143,13 +192,23 @@ def tile_koslmcell_pa_kernel(
             else:
                 nc.vector.quantize_mx(out=ch[i][:].bitcast(FP8X4), scales=sh[i][:], in_=gh[i][:])
 
-        def multiply(i, s, which):
+        def quantize_hh_part(i, s, g0=0, n=GH):
+            if i not in ch:
+                ch[i] = work.tile([P, 2 * GH * P], U32, name="ch", tag="ch", align_bytes=64)
+                sh[i] = work.tile([P, 2 * GH * P], U8, name="sh", tag="sh", align_bytes=64)
+            c0 = s * GH + g0
+            cols = slice(c0 * P, (c0 + n) * P)
+            nc.vector.quantize_mx(
+                out=ch[i][:, cols].bitcast(FP8X4), scales=sh[i][:, cols], in_=gh[i][:, c0 * 512 : (c0 + n) * 512]
+            )
+
+        def multiply(i, s, which, gs=None):
             if which == "x":
                 acc[i, s] = accp.tile([P, B], F32, name="acc%d" % s, tag="acc%d" % s)
                 wc, ws, ac, as_, n = ci[i], si[i], xq, xs, GX
             else:
                 wc, ws, ac, as_, n = ch[i], sh[i], hq, hs, GH
-            for g in range(n):
+            for g in gs if gs is not None else range(n):
                 wcol = s * n + g
                 nc.tensor.matmul_mx(
                     out=acc[i, s][:],
@@ -176,43 +235,68 @@ def tile_koslmcell_pa_kernel(
             )
 
         def store(i, k):
-            if i >= NU - 2:
-                nc.scalar.dma_start(out=out_views[k][:, :, i * P : (i + 1) * P], in_=st[k][:])
+            if i in ALONE:
+                nc.sync.dma_start(out=out_views[k][:, :, i * P : (i + 1) * P], in_=st[k, i // 2][:])
             elif i % 2 == 1:
-                nc.scalar.dma_start(out=out_views[k][:, :, (i - 1) * P : (i + 1) * P], in_=st[k][:])
+                nc.sync.dma_start(out=out_views[k][:, :, (i - 1) * P : (i + 1) * P], in_=st[k, i // 2][:])
+
+        def out_pe(i, parts="tzi"):
+            if i == LW and "t" in parts:
+                ott[i] = tp.tile([P, 4, P], F32, name="ot_t", tag="tp")
+            if i == LW and "z" in parts:
+                ot[i] = tp.tile([P, 4, P], F32, name="ot_z", tag="tp")
+            if i not in ot and i != LW:
+                ot[i] = otp.tile([P, 4, P], F32, name="ot_a", tag="ot_a")
+                ott[i] = ot[i]
+            if "t" in parts:
+                for bh in range(2):
+                    nc.tensor.transpose(ott[i][:, 2 + bh, :], tT[i][:, bh * P : (bh + 1) * P], ident_f[:])
+            if "z" in parts:
+                for bh in range(2):
+                    nc.tensor.transpose(ot[i][:, bh, :], zT[i][:, bh * P : (bh + 1) * P], ident_f[:])
+            if "i" in parts:
+                ob[i] = otp.tile([P, 2, P], F32, name="ot_b", tag="ot_b")
+                for bh in range(2):
+                    rows = slice(bh * P, (bh + 1) * P)
+                    nc.tensor.matmul(
+                        out=ob[i][:, bh, :], lhsT=zT[i][:, rows], rhs=ident_f[:], is_transpose=True, start=True, stop=False
+                    )
+                    nc.tensor.matmul(
+                        out=ob[i][:, bh, :], lhsT=prodT[i][:, rows], rhs=ident_f[:], is_transpose=True, start=False, stop=True
+                    )
+
+        def out_s(i, parts="tzi"):
+            alone = i in ALONE
+            half = 0 if alone else i % 2
+            if (0, i // 2) not in st or (alone and i not in started):
+                started.add(i)
+                for k in range(3):
+                    st[k, i // 2] = stage.tile([P, 2, P if alone else 2 * P], F32, name="st%d" % k, tag="st%d" % k)
+            cols = slice(half * P, (half + 1) * P)
+            if "t" in parts:
+                nc.scalar.activation(out=st[1, i // 2][:, :, cols], in_=ott[i][:, 2:4, :], func=ACT.Copy, scale=M_SCALE)
+                store(i, 1)
+            if "z" in parts:
+                nc.scalar.copy(out=st[0, i // 2][:, :, cols], in_=ot[i][:, 0:2, :])
+                store(i, 0)
+            if "i" in parts:
+                if i == LW:
+                    nc.vector.tensor_copy(out=st[2, i // 2][:, :, cols], in_=ob[i][:])
+                    nc.scalar.dma_start(out=out_views[2][:, :, i * P : (i + 1) * P], in_=st[2, i // 2][:])
+                else:
+                    nc.scalar.copy(out=st[2, i // 2][:, :, cols], in_=ob[i][:])
+                    store(i, 2)
 
         def outputs(i):
-            alone = i >= NU - 2
-            half = 0 if alone else i % 2
-            if half == 0:
-                for k in range(3):
-                    st[k] = stage.tile([P, 2, P if alone else 2 * P], F32, name="st%d" % k, tag="st%d" % k)
-            cols = slice(half * P, (half + 1) * P)
-            ot_a = otp.tile([P, 4, P], F32, name="ot_a", tag="ot_a")
-            for bh in range(2):
-                nc.tensor.transpose(ot_a[:, bh, :], zT[i][:, bh * P : (bh + 1) * P], ident_f[:])
-            for bh in range(2):
-                nc.tensor.transpose(ot_a[:, 2 + bh, :], tT[i][:, bh * P : (bh + 1) * P], ident_f[:])
-            nc.scalar.copy(out=st[0][:, :, cols], in_=ot_a[:, 0:2, :])
-            nc.scalar.activation(out=st[1][:, :, cols], in_=ot_a[:, 2:4, :], func=ACT.Copy, scale=M_SCALE)
-            for k in range(2):
-                store(i, k)
-            ot_b = otp.tile([P, 2, P], F32, name="ot_b", tag="ot_b")
-            for bh in range(2):
-                rows = slice(bh * P, (bh + 1) * P)
-                nc.tensor.matmul(
-                    out=ot_b[:, bh, :], lhsT=zT[i][:, rows], rhs=ident_f[:], is_transpose=True, start=True, stop=False
-                )
-                nc.tensor.matmul(
-                    out=ot_b[:, bh, :], lhsT=prodT[i][:, rows], rhs=ident_f[:], is_transpose=True, start=False, stop=True
-                )
-            nc.scalar.copy(out=st[2][:, :, cols], in_=ot_b[:])
-            store(i, 2)
+            out_pe(i, "tz")
+            out_s(i, "tz")
+            out_pe(i, "i")
+            out_s(i, "i")
 
         widen(0, [(H + c * 512, H + (c + 1) * 512, c * 512) for c in range(4)] + [(0, H, 0)])
         turn_hh(0, M)
         turn_hh(0, Z)
-        widen(1, [(H, 2 * H, 0), (0, H, 0)])
+        widen(1, [(0, 2 * H, 0)])
         widen(2, [(H, 2 * H, 0)])
 
         gx = const.tile([P, GX * B * 4], BF16, name="gx", align_bytes=64)
@@ -232,18 +316,16 @@ def tile_koslmcell_pa_kernel(
         nc.vector.quantize_mx(out=hq[:].bitcast(FP8X4), scales=hs[:], in_=ga[:])
 
         turn_ih(0)
-        vps = tp.tile([P, P], BF16, name="vps", tag="tp")
-        nc.tensor.transpose(vps[:], vrows[:], ident_b[:])
-        vT = const.tile([P, P], F32, name="vT")
-        nc.scalar.copy(out=vT[:], in_=vps[:])
-        lam = const.tile([P, NU], F32, name="lam")
-        nc.scalar.activation(out=lam[:], in_=vT[:, 96:112], func=ACT.Exp)
-        bias0 = const.tile([P, 2 * NU], F32, name="bias0")
-        nc.vector.tensor_tensor(out=bias0[:], in0=vT[:, 0:32], in1=vT[:, 32:64], op=ALU.add)
-        lam15 = const.tile([P, NU], F32, name="lam15")
-        nc.vector.tensor_scalar(out=lam15[:], in0=lam[:], scalar1=M_SCALE, scalar2=None, op0=ALU.mult)
+        vps = tp.tile([P, 3 * NU], F32, name="vps", tag="tp")
+        for a in range(3):
+            nc.tensor.matmul(
+                out=vps[:, 0 : 2 * NU], lhsT=vrows[:], rhs=ident_b[:, 32 * a : 32 * (a + 1)], start=(a == 0), stop=(a == 2)
+            )
+        nc.tensor.matmul(out=vps[:, 2 * NU : 3 * NU], lhsT=vrows[:], rhs=ident_b[:, 96:112], start=True, stop=True)
         bias = const.tile([P, 2 * NU], F32, name="bias")
-        nc.vector.tensor_tensor(out=bias[:], in0=bias0[:], in1=vT[:, 64:96], op=ALU.add)
+        nc.scalar.copy(out=bias[:], in_=vps[:, 0 : 2 * NU])
+        lam15 = const.tile([P, NU], F32, name="lam15")
+        nc.scalar.activation(out=lam15[:], in_=vps[:, 2 * NU : 3 * NU], func=ACT.Exp, bias=math.log(M_SCALE))
 
         turn_hh(1, M)
         turn_hh(1, Z)
@@ -261,61 +343,96 @@ def tile_koslmcell_pa_kernel(
                         nc.tensor.transpose(cps[:, j2, bh, :], c_sb[:, bh, j * P : (j + 1) * P], ident_b[:])
                 nc.scalar.copy(out=cT[:, 2 * jj : 2 * jj + 2, :], in_=cps[:].rearrange("p j bh b -> p j (bh b)"))
 
+        XPOS = 13
+        seq = list(range(XPOS)) + OFF + list(range(XPOS, LW + 1))
+        NS = len(seq)
+        sched = {}
+        for j in OFF:
+            groups = [[("cast", j, 0)]]
+            for g in range(GH):
+                groups.append([("turn", j, g)])
+                groups.append([("weave", j, g)] + ([("cast", j, g + 1)] if g + 1 < GH else []))
+            for n in range(len(groups)):
+                sched.setdefault(2 + (n * (12 - 2)) // len(groups), []).extend(groups[n])
+
         turn_ih(1)
-        last = NU - 1
-        for i in range(1, last):
+        for n in range(1, NS - 1):
+            i, i1, i2 = seq[n], seq[n - 1], seq[n - 2]
             if i == 2:
                 turn_hh(i, M)
                 widen(i, [(0, H, 0)])
                 turn_hh(i, Z)
-            elif i > 2:
+            elif i > 2 and i <= LW:
                 widen(i, [(0, 2 * H, 0)])
                 turn_hh(i, M)
                 turn_hh(i, Z)
-            if 1 < i and i + 3 < NU:
-                load_whb(i + 3)
-                load_wih(i + 3)
-            quantize_ih(i - 1)
-            quantize_hh(i - 1, False)
-            if i >= 2:
-                product(i - 2)
-            if i == 1:
+            if 1 < n and n + 3 < NS:
+                if seq[n + 3] <= LW:
+                    load_whb(seq[n + 3])
+                load_wih(seq[n + 3])
+            quantize_ih(i1)
+            quantize_hh(i1, False)
+            if n >= 2:
+                product(i2)
+            if n == 1:
                 turn_c(0, CT_FIRST)
-            multiply(i - 1, M, "x")
-            multiply(i - 1, M, "h")
-            tanh_m(i - 1)
-            turn_ih(i + 1)
-            multiply(i - 1, Z, "x")
-            multiply(i - 1, Z, "h")
-            tanh_z(i - 1)
-            if i == 1:
+            multiply(i1, M, "x")
+            multiply(i1, M, "h")
+            tanh_m(i1)
+            turn_ih(seq[n + 1])
+            now = sched.get(n, [])
+            for what, j, g in now:
+                if what == "turn":
+                    off_turn(j, g)
+            multiply(i1, Z, "x")
+            multiply(i1, Z, "h")
+            tanh_z(i1)
+            if n == 1:
                 turn_c(CT_FIRST, NU // 2 - CT_FIRST)
-            if i >= 2:
-                outputs(i - 2)
+            if n >= 2:
+                outputs(i2)
+            for what, j, g in now:
+                if what == "cast":
+                    off_cast(j, g)
+                elif what == "turn":
+                    off_scale(j, g)
+                else:
+                    off_weave(j, g)
 
-        widen(last, [(H, 2 * H, 0)])
-        turn_hh(last, M)
-        quantize_ih(last - 1)
-        quantize_hh(last - 1, False)
-        product(last - 2)
-        multiply(last - 1, M, "x")
-        multiply(last - 1, M, "h")
-        tanh_m(last - 1)
-        multiply(last - 1, Z, "x")
-        multiply(last - 1, Z, "h")
-        tanh_z(last - 1)
-        widen(last, [(0, H, 0)])
-        turn_hh(last, Z)
-        outputs(last - 2)
-        quantize_ih(last)
-        quantize_hh(last, True)
-        product(last - 1)
-        multiply(last, M, "x")
-        multiply(last, Z, "x")
-        multiply(last, M, "h")
-        tanh_m(last)
-        multiply(last, Z, "h")
-        tanh_z(last)
-        outputs(last - 1)
-        product(last)
-        outputs(last)
+        L, L1, L2 = seq[-1], seq[-2], seq[-3]
+        widen(L, [(H, 2 * H, 0)])
+        turn_hh(L, M)
+        quantize_ih(L1)
+        quantize_hh(L1, False)
+        product(L2)
+        multiply(L1, M, "x")
+        multiply(L1, M, "h")
+        tanh_m(L1)
+        multiply(L1, Z, "x")
+        multiply(L1, Z, "h")
+        tanh_z(L1)
+        widen(L, [(0, 1024, 0)])
+        turn_hh(L, Z, ((0, 2),))
+        outputs(L2)
+        quantize_ih(L)
+        quantize_hh_part(L, M)
+        multiply(L, M, "x")
+        multiply(L, M, "h")
+        tanh_m(L)
+        multiply(L, Z, "x")
+        widen(L, [(1024, 1536, 1024), (1536, 2048, 1536)])
+        turn_hh(L, Z, ((2, 1), (3, 1)))
+        product(L1)
+        out_pe(L1, "tzi")
+        quantize_hh_part(L, Z, 0, 2)
+        multiply(L, Z, "h", (0, 1))
+        out_s(L1, "tzi")
+        quantize_hh_part(L, Z, 2, 1)
+        quantize_hh_part(L, Z, 3, 1)
+        product(L)
+        out_pe(L, "t")
+        multiply(L, Z, "h", (2, 3))
+        tanh_z(L)
+        out_s(L, "t")
+        out_pe(L, "iz")
+        out_s(L, "iz")

@@ -379,14 +379,11 @@ def tile_koslmcell_pa_kernel(
             multiply(i1, M, "x")
             multiply(i1, M, "h")
             tanh_m(i1)
-            turn_ih(seq[n + 1])
-            now = sched.get(n, [])
-            for what, j, g in now:
-                if what == "turn":
-                    off_turn(j, g)
             multiply(i1, Z, "x")
             multiply(i1, Z, "h")
             tanh_z(i1)
+            turn_ih(seq[n + 1])
+            now = sched.get(n, [])
             if n == 1:
                 turn_c(CT_FIRST, NU // 2 - CT_FIRST)
             if n >= 2:

@@ -40,9 +40,8 @@ def tile_koslmcell_pa_kernel(
         work = ctx.enter_context(tc.tile_pool(name="work", bufs=3))
         stage = ctx.enter_context(tc.tile_pool(name="stage", bufs=3))
         offp = ctx.enter_context(tc.tile_pool(name="offp", bufs=2))
-        tp = ctx.enter_context(tc.psum_pool(name="tp", bufs=4))
+        tp = ctx.enter_context(tc.psum_pool(name="tp", bufs=6))
         accp = ctx.enter_context(tc.psum_pool(name="accp", bufs=1))
-        otp = ctx.enter_context(tc.psum_pool(name="otp", bufs=1))
         ctx.enter_context(tc.manual_schedule())
 
         whb_view = W_hh_bytes.rearrange("(s j p) k -> j p s k", s=2, p=P)
@@ -246,7 +245,7 @@ def tile_koslmcell_pa_kernel(
             if i == LW and "z" in parts:
                 ot[i] = tp.tile([P, 4, P], F32, name="ot_z", tag="tp")
             if i not in ot and i != LW:
-                ot[i] = otp.tile([P, 4, P], F32, name="ot_a", tag="ot_a")
+                ot[i] = tp.tile([P, 4, P], F32, name="ot_a", tag="tp")
                 ott[i] = ot[i]
             if "t" in parts:
                 for bh in range(2):
@@ -255,7 +254,7 @@ def tile_koslmcell_pa_kernel(
                 for bh in range(2):
                     nc.tensor.transpose(ot[i][:, bh, :], zT[i][:, bh * P : (bh + 1) * P], ident_f[:])
             if "i" in parts:
-                ob[i] = otp.tile([P, 2, P], F32, name="ot_b", tag="ot_b")
+                ob[i] = tp.tile([P, 2, P], F32, name="ot_b", tag="tp")
                 for bh in range(2):
                     rows = slice(bh * P, (bh + 1) * P)
                     nc.tensor.matmul(
@@ -408,28 +407,18 @@ def tile_koslmcell_pa_kernel(
         multiply(L1, Z, "x")
         multiply(L1, Z, "h")
         tanh_z(L1)
-        widen(L, [(0, 1024, 0)])
-        turn_hh(L, Z, ((0, 2),))
+        widen(L, [(0, H, 0)])
+        turn_hh(L, Z)
         outputs(L2)
         quantize_ih(L)
-        quantize_hh_part(L, M)
+        quantize_hh(L, True)
+        product(L1)
         multiply(L, M, "x")
+        multiply(L, Z, "x")
         multiply(L, M, "h")
         tanh_m(L)
-        multiply(L, Z, "x")
-        widen(L, [(1024, 1536, 1024), (1536, 2048, 1536)])
-        turn_hh(L, Z, ((2, 1), (3, 1)))
-        product(L1)
-        out_pe(L1, "tzi")
-        quantize_hh_part(L, Z, 0, 2)
-        multiply(L, Z, "h", (0, 1))
-        out_s(L1, "tzi")
-        quantize_hh_part(L, Z, 2, 1)
-        quantize_hh_part(L, Z, 3, 1)
-        product(L)
-        out_pe(L, "t")
-        multiply(L, Z, "h", (2, 3))
+        multiply(L, Z, "h")
         tanh_z(L)
-        out_s(L, "t")
-        out_pe(L, "iz")
-        out_s(L, "iz")
+        outputs(L1)
+        product(L)
+        outputs(L)

@@ -273,13 +273,21 @@ def tile_koslmcell_pa_kernel(
                     st[k, i // 2] = stage.tile([P, 2, P if alone else 2 * P], F32, name="st%d" % k, tag="st%d" % k)
             cols = slice(half * P, (half + 1) * P)
             if "t" in parts:
-                nc.scalar.activation(out=st[1, i // 2][:, :, cols], in_=ott[i][:, 2:4, :], func=ACT.Copy, scale=M_SCALE)
+                if i == LW:
+                    nc.vector.tensor_scalar(
+                        out=st[1, i // 2][:, :, cols], in0=ott[i][:, 2:4, :], scalar1=M_SCALE, scalar2=None, op0=ALU.mult
+                    )
+                else:
+                    nc.scalar.activation(out=st[1, i // 2][:, :, cols], in_=ott[i][:, 2:4, :], func=ACT.Copy, scale=M_SCALE)
                 store(i, 1)
             if "z" in parts:
                 nc.scalar.copy(out=st[0, i // 2][:, :, cols], in_=ot[i][:, 0:2, :])
                 store(i, 0)
             if "i" in parts:
-                if i == LW:
+                if i == LW - 1:
+                    nc.vector.tensor_copy(out=st[2, i // 2][:, :, cols], in_=ob[i][:])
+                    store(i, 2)
+                elif i == LW:
                     nc.vector.tensor_copy(out=st[2, i // 2][:, :, cols], in_=ob[i][:])
                     nc.scalar.dma_start(out=out_views[2][:, :, i * P : (i + 1) * P], in_=st[2, i // 2][:])
                 else:
@@ -383,8 +391,8 @@ def tile_koslmcell_pa_kernel(
             tanh_z(i1)
             turn_ih(seq[n + 1])
             now = sched.get(n, [])
-            if n == 1:
-                turn_c(CT_FIRST, NU // 2 - CT_FIRST)
+            if 1 <= n < NU // 2:
+                turn_c(n, 1)
             if n >= 2:
                 outputs(i2)
             for what, j, g in now:
@@ -417,8 +425,8 @@ def tile_koslmcell_pa_kernel(
         multiply(L, Z, "x")
         multiply(L, M, "h")
         tanh_m(L)
+        product(L)
         multiply(L, Z, "h")
         tanh_z(L)
         outputs(L1)
-        product(L)
         outputs(L)

@@ -22,12 +22,7 @@ GX = D // 512
 GH = H // 512
 M_SCALE = 1.5
 Z, M = 0, 1
-CT_FIRST = 1
-N_OFF = 0
-LW = NU - 1 - N_OFF
-OFF = list(range(LW + 1, NU))
-DIRECT = False
-ALONE = (NU - 2, NU - 1)
+LAST = NU - 1
 
 
 def tile_koslmcell_pa_kernel(
@@ -39,7 +34,6 @@ def tile_koslmcell_pa_kernel(
         loads = ctx.enter_context(tc.tile_pool(name="loads", bufs=4))
         work = ctx.enter_context(tc.tile_pool(name="work", bufs=3))
         stage = ctx.enter_context(tc.tile_pool(name="stage", bufs=3))
-        offp = ctx.enter_context(tc.tile_pool(name="offp", bufs=2))
         tp = ctx.enter_context(tc.psum_pool(name="tp", bufs=6))
         accp = ctx.enter_context(tc.psum_pool(name="accp", bufs=1))
         ctx.enter_context(tc.manual_schedule())
@@ -52,8 +46,6 @@ def tile_koslmcell_pa_kernel(
         whb, wih, wb, gh, gi = {}, {}, {}, {}, {}
         ch, sh, ci, si, acc = {}, {}, {}, {}, {}
         zT, tT, prodT, st = {}, {}, {}, {}
-        whbo, wbo, obank, pl = {}, {}, {}, {}
-        ot, ott, ob, started = {}, {}, {}, set()
 
         ident_f = const.tile([P, P], F32, name="ident_f")
         make_identity(nc, ident_f[:])
@@ -98,35 +90,32 @@ def tile_koslmcell_pa_kernel(
         nc.sync.dma_start(out=vrows[64:80, :], in_=z_bias.rearrange("(j p) -> j p", p=P))
         nc.sync.dma_start(out=vrows[80:96, :], in_=m_bias.rearrange("(j p) -> j p", p=P))
         nc.sync.dma_start(out=vrows[96:112, :], in_=log_lambda.rearrange("(j p) -> j p", p=P))
-        if OFF:
-            sT = const.tile([P, GH, 4], F32, name="sT")
-            nc.sync.dma_start(out=sT[:], in_=W_hh_scale.rearrange("o (g p t) -> p (o g) t", p=P, t=4))
         load_wih(1)
         c_sb = const.tile([P, 2, H], BF16, name="c_sb")
         nc.sync.dma_start(out=c_sb[:], in_=c_prev.rearrange("(bh p) n -> p bh n", p=P))
         load_whb(3)
         load_wih(2)
         load_wih(3)
-        for j in OFF:
-            whbo[j] = const.tile([P, 2, H], U8, name="whbo%d" % j)
-            nc.sync.dma_start(out=whbo[j][:], in_=whb_view[j])
-            gh[j] = const.tile([P, 2 * GH * 512], BF16, name="gho%d" % j, align_bytes=64)
 
-        def turn(words, g0, dst, n=2):
+        def turn(words, g0, dst):
             bank = tp.tile([P, 2, 2, P], F32, name="bank", tag="tp")
-            for gg in range(n):
+            for gg in range(2):
                 for u in range(2):
                     g = g0 + gg
                     nc.tensor.transpose(bank[:, gg, u, :], words[:, 256 * g + u : 256 * (g + 1) : 2], ident_f[:])
-            nc.scalar.copy(out=dst, in_=bank[:, 0:n].rearrange("p g u r -> p g r u"))
+            nc.scalar.copy(out=dst, in_=bank[:, 0:2].rearrange("p g u r -> p g r u"))
 
-        def widen(i, pieces):
+        def widen(i, first, end, scale_from):
             if i not in wb:
                 wb[i] = work.tile([P, 2 * H], BF16, name="wb", tag="wb")
-            src = whb[i][:].rearrange("p s k -> p (s k)").bitcast(FP8)
-            scl = sbc[:].rearrange("p s k -> p (s k)")
-            for a, b, sa in pieces:
-                nc.vector.tensor_tensor(out=wb[i][:, a:b], in0=src[:, a:b], in1=scl[:, sa : sa + b - a], op=ALU.mult)
+            codes = whb[i][:].rearrange("p s k -> p (s k)").bitcast(FP8)
+            scales = sbc[:].rearrange("p s k -> p (s k)")
+            nc.vector.tensor_tensor(
+                out=wb[i][:, first:end],
+                in0=codes[:, first:end],
+                in1=scales[:, scale_from : scale_from + end - first],
+                op=ALU.mult,
+            )
 
         def turn_ih(i):
             gi[i] = work.tile([P, 2 * GX * 512], BF16, name="gi", tag="gi", align_bytes=64)
@@ -134,80 +123,35 @@ def tile_koslmcell_pa_kernel(
                 dst = gi[i][:, s * 1024 : (s + 1) * 1024].bitcast(F32).rearrange("p (g r u) -> p g r u", g=2, u=2)
                 turn(wih[i][:, s, :].bitcast(F32), 0, dst)
 
-        def turn_hh(i, s, runs=((0, 2), (2, 2))):
+        def turn_hh(i, s, pairs=(0, 2)):
             if i not in gh:
                 gh[i] = work.tile([P, 2 * GH * 512], BF16, name="gh", tag="gh", align_bytes=64)
-            for g0, n in runs:
+            for g0 in pairs:
                 o = s * 2048 + g0 * 512
-                dst = gh[i][:, o : o + 512 * n].bitcast(F32).rearrange("p (g r u) -> p g r u", g=n, u=2)
-                turn(wb[i][:, s * H : (s + 1) * H].bitcast(F32), g0, dst, n)
-
-        def off_cast(j, g):
-            wbo[j, g] = offp.tile([P, 2, 512], BF16, name="wbo", tag="wbo")
-            for s in (M, Z):
-                nc.scalar.copy(out=wbo[j, g][:, s, :], in_=whbo[j][:, s, g * 512 : (g + 1) * 512].bitcast(FP8))
-
-        def off_turn(j, g):
-            obank[j, g] = tp.tile([P, 2, 2, P], F32, name="bank", tag="tp")
-            for s in (M, Z):
-                words = wbo[j, g][:, s, :].bitcast(F32)
-                for u in range(2):
-                    nc.tensor.transpose(obank[j, g][:, s, u, :], words[:, u : 256 : 2], ident_f[:])
-
-        def off_scale(j, g):
-            bv = obank[j, g][:].bitcast(BF16).rearrange("p s u (r e) -> p s u r e", e=2)
-            dst = gh[j][:].rearrange("p (s g r t) -> p s g r t", s=2, g=GH, t=4)
-            if not DIRECT:
-                pl[j, g] = offp.tile([P, 4, 2, P], BF16, name="pl", tag="pl")
-            for u in range(2):
-                for e in range(2):
-                    t = 2 * u + e
-                    nc.scalar.activation(
-                        out=dst[:, :, g, :, t] if DIRECT else pl[j, g][:, t, :, :],
-                        in_=bv[:, :, u, :, e],
-                        func=ACT.Copy,
-                        scale=sT[:, g, t : t + 1],
-                    )
-
-        def off_weave(j, g):
-            if not DIRECT:
-                dst = gh[j][:].rearrange("p (s g r t) -> p s g r t", s=2, g=GH, t=4)
-                nc.scalar.copy(out=dst[:, :, g, :, :], in_=pl[j, g][:].rearrange("p t s r -> p s r t"))
+                dst = gh[i][:, o : o + 1024].bitcast(F32).rearrange("p (g r u) -> p g r u", g=2, u=2)
+                turn(wb[i][:, s * H : (s + 1) * H].bitcast(F32), g0, dst)
 
         def quantize_ih(i):
             ci[i] = work.tile([P, 2 * GX * P], U32, name="ci", tag="ci", align_bytes=64)
             si[i] = work.tile([P, 2 * GX * P], U8, name="si", tag="si", align_bytes=64)
             nc.vector.quantize_mx(out=ci[i][:].bitcast(FP8X4), scales=si[i][:], in_=gi[i][:])
 
-        def quantize_hh(i, split):
-            ch[i] = work.tile([P, 2 * GH * P], U32, name="ch", tag="ch", align_bytes=64)
-            sh[i] = work.tile([P, 2 * GH * P], U8, name="sh", tag="sh", align_bytes=64)
-            if split:
-                for s in (M, Z):
-                    cols = slice(s * GH * P, (s + 1) * GH * P)
-                    nc.vector.quantize_mx(
-                        out=ch[i][:, cols].bitcast(FP8X4), scales=sh[i][:, cols], in_=gh[i][:, s * 2048 : (s + 1) * 2048]
-                    )
-            else:
-                nc.vector.quantize_mx(out=ch[i][:].bitcast(FP8X4), scales=sh[i][:], in_=gh[i][:])
-
-        def quantize_hh_part(i, s, g0=0, n=GH):
+        def quantize_hh(i, first=0, count=2 * GH):
             if i not in ch:
                 ch[i] = work.tile([P, 2 * GH * P], U32, name="ch", tag="ch", align_bytes=64)
                 sh[i] = work.tile([P, 2 * GH * P], U8, name="sh", tag="sh", align_bytes=64)
-            c0 = s * GH + g0
-            cols = slice(c0 * P, (c0 + n) * P)
+            cols = slice(first * P, (first + count) * P)
             nc.vector.quantize_mx(
-                out=ch[i][:, cols].bitcast(FP8X4), scales=sh[i][:, cols], in_=gh[i][:, c0 * 512 : (c0 + n) * 512]
+                out=ch[i][:, cols].bitcast(FP8X4), scales=sh[i][:, cols], in_=gh[i][:, first * 512 : (first + count) * 512]
             )
 
-        def multiply(i, s, which, gs=None):
+        def multiply(i, s, which):
             if which == "x":
                 acc[i, s] = accp.tile([P, B], F32, name="acc%d" % s, tag="acc%d" % s)
                 wc, ws, ac, as_, n = ci[i], si[i], xq, xs, GX
             else:
                 wc, ws, ac, as_, n = ch[i], sh[i], hq, hs, GH
-            for g in gs if gs is not None else range(n):
+            for g in range(n):
                 wcol = s * n + g
                 nc.tensor.matmul_mx(
                     out=acc[i, s][:],
@@ -227,6 +171,14 @@ def tile_koslmcell_pa_kernel(
             zT[i] = work.tile([P, B], F32, name="zT", tag="zT")
             nc.scalar.activation(out=zT[i][:], in_=acc[i, Z][:], func=ACT.Tanh, bias=bias[:, i : i + 1])
 
+        def passes(i):
+            multiply(i, M, "x")
+            multiply(i, M, "h")
+            tanh_m(i)
+            multiply(i, Z, "x")
+            multiply(i, Z, "h")
+            tanh_z(i)
+
         def product(i):
             prodT[i] = work.tile([P, B], F32, name="prodT", tag="prodT")
             nc.vector.scalar_tensor_tensor(
@@ -234,77 +186,62 @@ def tile_koslmcell_pa_kernel(
             )
 
         def store(i, k):
-            if i in ALONE:
+            if i >= LAST - 1:
                 nc.sync.dma_start(out=out_views[k][:, :, i * P : (i + 1) * P], in_=st[k, i // 2][:])
             elif i % 2 == 1:
                 nc.sync.dma_start(out=out_views[k][:, :, (i - 1) * P : (i + 1) * P], in_=st[k, i // 2][:])
 
-        def out_pe(i, parts="tzi"):
-            if i == LW and "t" in parts:
-                ott[i] = tp.tile([P, 4, P], F32, name="ot_t", tag="tp")
-            if i == LW and "z" in parts:
-                ot[i] = tp.tile([P, 4, P], F32, name="ot_z", tag="tp")
-            if i not in ot and i != LW:
-                ot[i] = tp.tile([P, 4, P], F32, name="ot_a", tag="tp")
-                ott[i] = ot[i]
-            if "t" in parts:
-                for bh in range(2):
-                    nc.tensor.transpose(ott[i][:, 2 + bh, :], tT[i][:, bh * P : (bh + 1) * P], ident_f[:])
-            if "z" in parts:
-                for bh in range(2):
-                    nc.tensor.transpose(ot[i][:, bh, :], zT[i][:, bh * P : (bh + 1) * P], ident_f[:])
-            if "i" in parts:
-                ob[i] = tp.tile([P, 2, P], F32, name="ot_b", tag="tp")
-                for bh in range(2):
-                    rows = slice(bh * P, (bh + 1) * P)
-                    nc.tensor.matmul(
-                        out=ob[i][:, bh, :], lhsT=zT[i][:, rows], rhs=ident_f[:], is_transpose=True, start=True, stop=False
-                    )
-                    nc.tensor.matmul(
-                        out=ob[i][:, bh, :], lhsT=prodT[i][:, rows], rhs=ident_f[:], is_transpose=True, start=False, stop=True
-                    )
-
-        def out_s(i, parts="tzi"):
-            alone = i in ALONE
-            half = 0 if alone else i % 2
-            if (0, i // 2) not in st or (alone and i not in started):
-                started.add(i)
+        def finish(i):
+            alone = i >= LAST - 1
+            if i == LAST:
+                bank_t = tp.tile([P, 4, P], F32, name="ot_t", tag="tp")
+                bank_z = tp.tile([P, 4, P], F32, name="ot_z", tag="tp")
+            else:
+                bank_z = tp.tile([P, 4, P], F32, name="ot_a", tag="tp")
+                bank_t = bank_z
+            for bh in range(2):
+                nc.tensor.transpose(bank_t[:, 2 + bh, :], tT[i][:, bh * P : (bh + 1) * P], ident_f[:])
+            for bh in range(2):
+                nc.tensor.transpose(bank_z[:, bh, :], zT[i][:, bh * P : (bh + 1) * P], ident_f[:])
+            if alone or i % 2 == 0:
                 for k in range(3):
                     st[k, i // 2] = stage.tile([P, 2, P if alone else 2 * P], F32, name="st%d" % k, tag="st%d" % k)
+            half = 0 if alone else i % 2
             cols = slice(half * P, (half + 1) * P)
-            if "t" in parts:
-                if i == LW:
-                    nc.vector.tensor_scalar(
-                        out=st[1, i // 2][:, :, cols], in0=ott[i][:, 2:4, :], scalar1=M_SCALE, scalar2=None, op0=ALU.mult
-                    )
-                else:
-                    nc.scalar.activation(out=st[1, i // 2][:, :, cols], in_=ott[i][:, 2:4, :], func=ACT.Copy, scale=M_SCALE)
-                store(i, 1)
-            if "z" in parts:
-                nc.scalar.copy(out=st[0, i // 2][:, :, cols], in_=ot[i][:, 0:2, :])
-                store(i, 0)
-            if "i" in parts:
-                if i == LW - 1:
-                    nc.vector.tensor_copy(out=st[2, i // 2][:, :, cols], in_=ob[i][:])
-                    store(i, 2)
-                elif i == LW:
-                    nc.vector.tensor_copy(out=st[2, i // 2][:, :, cols], in_=ob[i][:])
-                    nc.scalar.dma_start(out=out_views[2][:, :, i * P : (i + 1) * P], in_=st[2, i // 2][:])
-                else:
-                    nc.scalar.copy(out=st[2, i // 2][:, :, cols], in_=ob[i][:])
-                    store(i, 2)
+            if i == LAST:
+                nc.vector.tensor_scalar(
+                    out=st[1, i // 2][:, :, cols], in0=bank_t[:, 2:4, :], scalar1=M_SCALE, scalar2=None, op0=ALU.mult
+                )
+            else:
+                nc.scalar.activation(out=st[1, i // 2][:, :, cols], in_=bank_t[:, 2:4, :], func=ACT.Copy, scale=M_SCALE)
+            store(i, 1)
+            nc.scalar.copy(out=st[0, i // 2][:, :, cols], in_=bank_z[:, 0:2, :])
+            store(i, 0)
+            bank_i = tp.tile([P, 2, P], F32, name="ot_b", tag="tp")
+            for bh in range(2):
+                rows = slice(bh * P, (bh + 1) * P)
+                nc.tensor.matmul(
+                    out=bank_i[:, bh, :], lhsT=zT[i][:, rows], rhs=ident_f[:], is_transpose=True, start=True, stop=False
+                )
+                nc.tensor.matmul(
+                    out=bank_i[:, bh, :], lhsT=prodT[i][:, rows], rhs=ident_f[:], is_transpose=True, start=False, stop=True
+                )
+            if alone:
+                nc.vector.tensor_copy(out=st[2, i // 2][:, :, cols], in_=bank_i[:])
+            else:
+                nc.scalar.copy(out=st[2, i // 2][:, :, cols], in_=bank_i[:])
+            if i == LAST:
+                nc.scalar.dma_start(out=out_views[2][:, :, i * P : (i + 1) * P], in_=st[2, i // 2][:])
+            else:
+                store(i, 2)
 
-        def outputs(i):
-            out_pe(i, "tz")
-            out_s(i, "tz")
-            out_pe(i, "i")
-            out_s(i, "i")
-
-        widen(0, [(H + c * 512, H + (c + 1) * 512, c * 512) for c in range(4)] + [(0, H, 0)])
+        for c in range(4):
+            widen(0, H + c * 512, H + (c + 1) * 512, c * 512)
+        widen(0, 0, H, 0)
         turn_hh(0, M)
         turn_hh(0, Z)
-        widen(1, [(0, 2 * H, 0)])
-        widen(2, [(H, 2 * H, 0)])
+        widen(1, 0, 2 * H, 0)
+        widen(2, H, 2 * H, 0)
 
         gx = const.tile([P, GX * B * 4], BF16, name="gx", align_bytes=64)
         gxw = gx[:].bitcast(F32).rearrange("p (g b u) -> p g b u", g=GX, u=2)
@@ -341,92 +278,62 @@ def tile_koslmcell_pa_kernel(
 
         cT = const.tile([P, NU, B], BF16, name="cT")
 
-        def turn_c(first, count):
-            for jj in range(first, first + count):
-                cps = tp.tile([P, 2, 2, P], BF16, name="cps", tag="tp")
-                for j2 in range(2):
-                    for bh in range(2):
-                        j = 2 * jj + j2
-                        nc.tensor.transpose(cps[:, j2, bh, :], c_sb[:, bh, j * P : (j + 1) * P], ident_b[:])
-                nc.scalar.copy(out=cT[:, 2 * jj : 2 * jj + 2, :], in_=cps[:].rearrange("p j bh b -> p j (bh b)"))
-
-        XPOS = 13
-        seq = list(range(XPOS)) + OFF + list(range(XPOS, LW + 1))
-        NS = len(seq)
-        sched = {}
-        for j in OFF:
-            groups = [[("cast", j, 0)]]
-            for g in range(GH):
-                groups.append([("turn", j, g)])
-                groups.append([("weave", j, g)] + ([("cast", j, g + 1)] if g + 1 < GH else []))
-            for n in range(len(groups)):
-                sched.setdefault(2 + (n * (12 - 2)) // len(groups), []).extend(groups[n])
+        def turn_c(jj):
+            cps = tp.tile([P, 2, 2, P], BF16, name="cps", tag="tp")
+            for j2 in range(2):
+                for bh in range(2):
+                    j = 2 * jj + j2
+                    nc.tensor.transpose(cps[:, j2, bh, :], c_sb[:, bh, j * P : (j + 1) * P], ident_b[:])
+            nc.scalar.copy(out=cT[:, 2 * jj : 2 * jj + 2, :], in_=cps[:].rearrange("p j bh b -> p j (bh b)"))
 
         turn_ih(1)
-        for n in range(1, NS - 1):
-            i, i1, i2 = seq[n], seq[n - 1], seq[n - 2]
-            if i == 2:
-                turn_hh(i, M)
-                widen(i, [(0, H, 0)])
-                turn_hh(i, Z)
-            elif i > 2 and i <= LW:
-                widen(i, [(0, 2 * H, 0)])
-                turn_hh(i, M)
-                turn_hh(i, Z)
-            if 1 < n and n + 3 < NS:
-                if seq[n + 3] <= LW:
-                    load_whb(seq[n + 3])
-                load_wih(seq[n + 3])
-            quantize_ih(i1)
-            quantize_hh(i1, False)
+        for n in range(1, LAST):
+            turn_ih(n + 1)
+            if n == 2:
+                turn_hh(n, M)
+                widen(n, 0, H, 0)
+                turn_hh(n, Z)
+            elif n > 2:
+                widen(n, 0, 2 * H, 0)
+                turn_hh(n, M)
+                turn_hh(n, Z)
+            if 1 < n and n + 3 < NU:
+                load_whb(n + 3)
+                load_wih(n + 3)
+            quantize_ih(n - 1)
+            quantize_hh(n - 1)
             if n >= 2:
-                product(i2)
+                product(n - 2)
             if n == 1:
-                turn_c(0, CT_FIRST)
-            multiply(i1, M, "x")
-            multiply(i1, M, "h")
-            tanh_m(i1)
-            multiply(i1, Z, "x")
-            multiply(i1, Z, "h")
-            tanh_z(i1)
-            turn_ih(seq[n + 1])
-            now = sched.get(n, [])
-            if 1 <= n < NU // 2:
-                turn_c(n, 1)
+                turn_c(0)
+            passes(n - 1)
+            if n < NU // 2:
+                turn_c(n)
             if n >= 2:
-                outputs(i2)
-            for what, j, g in now:
-                if what == "cast":
-                    off_cast(j, g)
-                elif what == "turn":
-                    off_scale(j, g)
-                else:
-                    off_weave(j, g)
+                finish(n - 2)
 
-        L, L1, L2 = seq[-1], seq[-2], seq[-3]
-        widen(L, [(H, 2 * H, 0)])
-        turn_hh(L, M)
-        quantize_ih(L1)
-        quantize_hh(L1, False)
-        product(L2)
-        multiply(L1, M, "x")
-        multiply(L1, M, "h")
-        tanh_m(L1)
-        multiply(L1, Z, "x")
-        multiply(L1, Z, "h")
-        tanh_z(L1)
-        widen(L, [(0, H, 0)])
-        turn_hh(L, Z)
-        outputs(L2)
-        quantize_ih(L)
-        quantize_hh(L, True)
-        product(L1)
-        multiply(L, M, "x")
-        multiply(L, Z, "x")
-        multiply(L, M, "h")
-        tanh_m(L)
-        product(L)
-        multiply(L, Z, "h")
-        tanh_z(L)
-        outputs(L1)
-        outputs(L)
+        widen(LAST, H, 2 * H, 0)
+        turn_hh(LAST, M)
+        quantize_ih(LAST - 1)
+        quantize_hh(LAST - 1)
+        product(LAST - 2)
+        passes(LAST - 1)
+        widen(LAST, 0, H // 2, 0)
+        turn_hh(LAST, Z, (0,))
+        widen(LAST, H // 2, H, H // 2)
+        turn_hh(LAST, Z, (2,))
+        finish(LAST - 2)
+        quantize_ih(LAST)
+        quantize_hh(LAST, GH, GH)
+        quantize_hh(LAST, 0, 2)
+        product(LAST - 1)
+        quantize_hh(LAST, 2, 2)
+        multiply(LAST, M, "x")
+        multiply(LAST, Z, "x")
+        multiply(LAST, M, "h")
+        tanh_m(LAST)
+        product(LAST)
+        multiply(LAST, Z, "h")
+        tanh_z(LAST)
+        finish(LAST - 1)
+        finish(LAST)

@@ -288,7 +288,6 @@ def tile_koslmcell_pa_kernel(
 
         turn_ih(1)
         for n in range(1, LAST):
-            turn_ih(n + 1)
             if n == 2:
                 turn_hh(n, M)
                 widen(n, 0, H, 0)
@@ -307,6 +306,7 @@ def tile_koslmcell_pa_kernel(
             if n == 1:
                 turn_c(0)
             passes(n - 1)
+            turn_ih(n + 1)
             if n < NU // 2:
                 turn_c(n)
             if n >= 2:

@@ -291,22 +291,27 @@ def tile_koslmcell_pa_kernel(
             if n == 2:
                 turn_hh(n, M)
                 widen(n, 0, H, 0)
-                turn_hh(n, Z)
             elif n > 2:
                 widen(n, 0, 2 * H, 0)
                 turn_hh(n, M)
-                turn_hh(n, Z)
             if 1 < n and n + 3 < NU:
                 load_whb(n + 3)
                 load_wih(n + 3)
+            if n == 1:
+                turn_c(0)
             quantize_ih(n - 1)
+            multiply(n - 1, M, "x")
+            multiply(n - 1, Z, "x")
+            if n >= 2:
+                turn_hh(n, Z)
             quantize_hh(n - 1)
             if n >= 2:
                 product(n - 2)
-            if n == 1:
-                turn_c(0)
-            passes(n - 1)
+            multiply(n - 1, M, "h")
+            tanh_m(n - 1)
             turn_ih(n + 1)
+            multiply(n - 1, Z, "h")
+            tanh_z(n - 1)
             if n < NU // 2:
                 turn_c(n)
             if n >= 2:

@@ -310,12 +310,12 @@ def tile_koslmcell_pa_kernel(
             multiply(n - 1, M, "h")
             tanh_m(n - 1)
             turn_ih(n + 1)
-            multiply(n - 1, Z, "h")
-            tanh_z(n - 1)
             if n < NU // 2:
                 turn_c(n)
             if n >= 2:
                 finish(n - 2)
+            multiply(n - 1, Z, "h")
+            tanh_z(n - 1)
 
         widen(LAST, H, 2 * H, 0)
         turn_hh(LAST, M)

@@ -68,14 +68,13 @@ def tile_koslmcell_pa_kernel(
 
         sbc = const.tile([P, 2, H], F32, name="sbc")
         whb[0] = loads.tile([P, 2, H], U8, name="whb", tag="whb")
-        nc.sync.dma_start(out=whb[0][:, M, 0:512], in_=whb_view[0][:, M, 0:512])
+        nc.sync.dma_start(out=whb[0][:, :, 0:512], in_=whb_view[0][:, :, 0:512])
         nc.sync.dma_start(out=sbc[:, 0, 0:512], in_=scale_row[0:512].partition_broadcast(P))
-        nc.sync.dma_start(out=whb[0][:, M, 512:H], in_=whb_view[0][:, M, 512:H])
+        nc.sync.dma_start(out=whb[0][:, :, 512:H], in_=whb_view[0][:, :, 512:H])
         for c in range(1, 4):
             nc.sync.dma_start(
                 out=sbc[:, 0, c * 512 : (c + 1) * 512], in_=scale_row[c * 512 : (c + 1) * 512].partition_broadcast(P)
             )
-        nc.sync.dma_start(out=whb[0][:, Z, :], in_=whb_view[0][:, Z, :])
         for c in range(4):
             nc.scalar.copy(out=sbc[:, 1, c * 512 : (c + 1) * 512], in_=sbc[:, 0, c * 512 : (c + 1) * 512])
         load_whb(1)
@@ -236,8 +235,8 @@ def tile_koslmcell_pa_kernel(
                 store(i, 2)
 
         for c in range(4):
-            widen(0, H + c * 512, H + (c + 1) * 512, c * 512)
-        widen(0, 0, H, 0)
+            for s in (M, Z):
+                widen(0, s * H + c * 512, s * H + (c + 1) * 512, c * 512)
         turn_hh(0, M)
         turn_hh(0, Z)
         widen(1, 0, 2 * H, 0)

import math
from contextlib import ExitStack

import concourse.mybir as mybir
from concourse.masks import make_identity

B, D, H = 256, 1024, 2048
FLOPS = 2 * B * (2 * H) * (D + H)

F32 = mybir.dt.float32
BF16 = mybir.dt.bfloat16
U32 = mybir.dt.uint32
U8 = mybir.dt.uint8
FP8 = mybir.dt.float8_e4m3fn
FP8X4 = mybir.dt.float8_e4m3fn_x4
ACT = mybir.ActivationFunctionType
ALU = mybir.AluOpType

P = 128
NU = H // P
GX = D // 512
GH = H // 512
M_SCALE = 1.5
Z, M = 0, 1
LAST = NU - 1


def tile_koslmcell_pa_kernel(
    tc, x, h_prev, c_prev, W_ih, b_ih, W_hh_bytes, W_hh_scale, b_hh, log_lambda, z_bias, m_bias, out_0, out_1, out_2
):
    nc = tc.nc
    with ExitStack() as ctx:
        const = ctx.enter_context(tc.tile_pool(name="const", bufs=1))
        loads = ctx.enter_context(tc.tile_pool(name="loads", bufs=4))
        work = ctx.enter_context(tc.tile_pool(name="work", bufs=3))
        stage = ctx.enter_context(tc.tile_pool(name="stage", bufs=3))
        tp = ctx.enter_context(tc.psum_pool(name="tp", bufs=6))
        accp = ctx.enter_context(tc.psum_pool(name="accp", bufs=1))
        ctx.enter_context(tc.manual_schedule())

        whb_view = W_hh_bytes.rearrange("(s j p) k -> j p s k", s=2, p=P)
        wih_view = W_ih.rearrange("(s j p) k -> j p s k", s=2, p=P)
        out_views = [o.rearrange("(bh p) n -> p bh n", p=P) for o in (out_0, out_1, out_2)]
        scale_row = W_hh_scale.rearrange("o k -> (o k)")

        whb, wih, wb, gh, gi = {}, {}, {}, {}, {}
        ch, sh, ci, si, acc = {}, {}, {}, {}, {}
        zT, tT, prodT, st = {}, {}, {}, {}

        ident_f = const.tile([P, P], F32, name="ident_f")
        make_identity(nc, ident_f[:])
        ident_b = const.tile([P, P], BF16, name="ident_b")
        make_identity(nc, ident_b[:])
        warm = const.tile([P, 1], F32, name="warm")
        nc.vector.memset(warm[:], 0.0)
        warm2 = const.tile([P, 1], F32, name="warm2")
        nc.scalar.activation(out=warm2[:], in_=warm[:], func=ACT.Tanh)
        vrows = const.tile([P, P], BF16, name="vrows")
        nc.vector.memset(vrows[:], 0.0)

        def load_whb(i):
            whb[i] = loads.tile([P, 2, H], U8, name="whb", tag="whb")
            nc.sync.dma_start(out=whb[i][:], in_=whb_view[i])

        def load_wih(i):
            wih[i] = loads.tile([P, 2, D], BF16, name="wih", tag="wih")
            nc.sync.dma_start(out=wih[i][:], in_=wih_view[i])

        sbc = const.tile([P, 2, H], F32, name="sbc")
        whb[0] = loads.tile([P, 2, H], U8, name="whb", tag="whb")
        nc.sync.dma_start(out=whb[0][:, :, 0:512], in_=whb_view[0][:, :, 0:512])
        nc.sync.dma_start(out=sbc[:, 0, 0:512], in_=scale_row[0:512].partition_broadcast(P))
        nc.sync.dma_start(out=whb[0][:, :, 512:H], in_=whb_view[0][:, :, 512:H])
        for c in range(1, 4):
            nc.sync.dma_start(
                out=sbc[:, 0, c * 512 : (c + 1) * 512], in_=scale_row[c * 512 : (c + 1) * 512].partition_broadcast(P)
            )
        for c in range(4):
            nc.scalar.copy(out=sbc[:, 1, c * 512 : (c + 1) * 512], in_=sbc[:, 0, c * 512 : (c + 1) * 512])
        load_whb(1)
        x_sb = const.tile([P, 2, D], BF16, name="x_sb")
        nc.sync.dma_start(out=x_sb[:], in_=x.rearrange("(bt p) k -> p bt k", p=P))
        h_sb = const.tile([P, 2, H], BF16, name="h_sb")
        nc.sync.dma_start(out=h_sb[:], in_=h_prev.rearrange("(bt p) k -> p bt k", p=P))
        load_whb(2)
        load_wih(0)
        nc.sync.dma_start(out=vrows[0:32, :], in_=b_ih.rearrange("(j p) -> j p", p=P))
        nc.sync.dma_start(out=vrows[32:64, :], in_=b_hh.rearrange("(j p) -> j p", p=P))
        nc.sync.dma_start(out=vrows[64:80, :], in_=z_bias.rearrange("(j p) -> j p", p=P))
        nc.sync.dma_start(out=vrows[80:96, :], in_=m_bias.rearrange("(j p) -> j p", p=P))
        nc.sync.dma_start(out=vrows[96:112, :], in_=log_lambda.rearrange("(j p) -> j p", p=P))
        load_wih(1)
        c_sb = const.tile([P, 2, H], BF16, name="c_sb")
        nc.sync.dma_start(out=c_sb[:], in_=c_prev.rearrange("(bh p) n -> p bh n", p=P))
        load_whb(3)
        load_wih(2)
        load_wih(3)

        def turn(words, g0, dst):
            bank = tp.tile([P, 2, 2, P], F32, name="bank", tag="tp")
            for gg in range(2):
                for u in range(2):
                    g = g0 + gg
                    nc.tensor.transpose(bank[:, gg, u, :], words[:, 256 * g + u : 256 * (g + 1) : 2], ident_f[:])
            nc.scalar.copy(out=dst, in_=bank[:, 0:2].rearrange("p g u r -> p g r u"))

        def widen(i, first, end, scale_from):
            if i not in wb:
                wb[i] = work.tile([P, 2 * H], BF16, name="wb", tag="wb")
            codes = whb[i][:].rearrange("p s k -> p (s k)").bitcast(FP8)
            scales = sbc[:].rearrange("p s k -> p (s k)")
            nc.vector.tensor_tensor(
                out=wb[i][:, first:end],
                in0=codes[:, first:end],
                in1=scales[:, scale_from : scale_from + end - first],
                op=ALU.mult,
            )

        def turn_ih(i):
            gi[i] = work.tile([P, 2 * GX * 512], BF16, name="gi", tag="gi", align_bytes=64)
            for s in (M, Z):
                dst = gi[i][:, s * 1024 : (s + 1) * 1024].bitcast(F32).rearrange("p (g r u) -> p g r u", g=2, u=2)
                turn(wih[i][:, s, :].bitcast(F32), 0, dst)

        def turn_hh(i, s, pairs=(0, 2)):
            if i not in gh:
                gh[i] = work.tile([P, 2 * GH * 512], BF16, name="gh", tag="gh", align_bytes=64)
            for g0 in pairs:
                o = s * 2048 + g0 * 512
                dst = gh[i][:, o : o + 1024].bitcast(F32).rearrange("p (g r u) -> p g r u", g=2, u=2)
                turn(wb[i][:, s * H : (s + 1) * H].bitcast(F32), g0, dst)

        def quantize_ih(i):
            ci[i] = work.tile([P, 2 * GX * P], U32, name="ci", tag="ci", align_bytes=64)
            si[i] = work.tile([P, 2 * GX * P], U8, name="si", tag="si", align_bytes=64)
            nc.vector.quantize_mx(out=ci[i][:].bitcast(FP8X4), scales=si[i][:], in_=gi[i][:])

        def quantize_hh(i, first=0, count=2 * GH):
            if i not in ch:
                ch[i] = work.tile([P, 2 * GH * P], U32, name="ch", tag="ch", align_bytes=64)
                sh[i] = work.tile([P, 2 * GH * P], U8, name="sh", tag="sh", align_bytes=64)
            cols = slice(first * P, (first + count) * P)
            nc.vector.quantize_mx(
                out=ch[i][:, cols].bitcast(FP8X4), scales=sh[i][:, cols], in_=gh[i][:, first * 512 : (first + count) * 512]
            )

        def multiply(i, s, which):
            if which == "x":
                acc[i, s] = accp.tile([P, B], F32, name="acc%d" % s, tag="acc%d" % s)
                wc, ws, ac, as_, n = ci[i], si[i], xq, xs, GX
            else:
                wc, ws, ac, as_, n = ch[i], sh[i], hq, hs, GH
            for g in range(n):
                wcol = s * n + g
                nc.tensor.matmul_mx(
                    out=acc[i, s][:],
                    lhsT=wc[:, wcol * P : (wcol + 1) * P].bitcast(FP8X4),
                    lhsT_scale=ws[:, wcol * P : (wcol + 1) * P],
                    rhs=ac[:, g * B : (g + 1) * B].bitcast(FP8X4),
                    rhs_scale=as_[:, g * B : (g + 1) * B],
                    start=(which == "x" and g == 0),
                    stop=(which == "h" and g == n - 1),
                )

        def tanh_m(i):
            tT[i] = work.tile([P, B], F32, name="tT", tag="tT")
            nc.scalar.activation(out=tT[i][:], in_=acc[i, M][:], func=ACT.Tanh, bias=bias[:, NU + i : NU + i + 1])

        def tanh_z(i):
            zT[i] = work.tile([P, B], F32, name="zT", tag="zT")
            nc.scalar.activation(out=zT[i][:], in_=acc[i, Z][:], func=ACT.Tanh, bias=bias[:, i : i + 1])

        def passes(i):
            multiply(i, M, "x")
            multiply(i, M, "h")
            tanh_m(i)
            multiply(i, Z, "x")
            multiply(i, Z, "h")
            tanh_z(i)

        def product(i):
            prodT[i] = work.tile([P, B], F32, name="prodT", tag="prodT")
            nc.vector.scalar_tensor_tensor(
                out=prodT[i][:], in0=tT[i][:], scalar=lam15[:, i : i + 1], in1=cT[:, i, :], op0=ALU.mult, op1=ALU.mult
            )

        def store(i, k):
            if i >= LAST - 1:
                nc.sync.dma_start(out=out_views[k][:, :, i * P : (i + 1) * P], in_=st[k, i // 2][:])
            elif i % 2 == 1:
                nc.sync.dma_start(out=out_views[k][:, :, (i - 1) * P : (i + 1) * P], in_=st[k, i // 2][:])

        def finish(i):
            alone = i >= LAST - 1
            if i == LAST:
                bank_t = tp.tile([P, 4, P], F32, name="ot_t", tag="tp")
                bank_z = tp.tile([P, 4, P], F32, name="ot_z", tag="tp")
            else:
                bank_z = tp.tile([P, 4, P], F32, name="ot_a", tag="tp")
                bank_t = bank_z
            for bh in range(2):
                nc.tensor.transpose(bank_t[:, 2 + bh, :], tT[i][:, bh * P : (bh + 1) * P], ident_f[:])
            for bh in range(2):
                nc.tensor.transpose(bank_z[:, bh, :], zT[i][:, bh * P : (bh + 1) * P], ident_f[:])
            if alone or i % 2 == 0:
                for k in range(3):
                    st[k, i // 2] = stage.tile([P, 2, P if alone else 2 * P], F32, name="st%d" % k, tag="st%d" % k)
            half = 0 if alone else i % 2
            cols = slice(half * P, (half + 1) * P)
            if i == LAST:
                nc.vector.tensor_scalar(
                    out=st[1, i // 2][:, :, cols], in0=bank_t[:, 2:4, :], scalar1=M_SCALE, scalar2=None, op0=ALU.mult
                )
            else:
                nc.scalar.activation(out=st[1, i // 2][:, :, cols], in_=bank_t[:, 2:4, :], func=ACT.Copy, scale=M_SCALE)
            store(i, 1)
            nc.scalar.copy(out=st[0, i // 2][:, :, cols], in_=bank_z[:, 0:2, :])
            store(i, 0)
            bank_i = tp.tile([P, 2, P], F32, name="ot_b", tag="tp")
            for bh in range(2):
                rows = slice(bh * P, (bh + 1) * P)
                nc.tensor.matmul(
                    out=bank_i[:, bh, :], lhsT=zT[i][:, rows], rhs=ident_f[:], is_transpose=True, start=True, stop=False
                )
                nc.tensor.matmul(
                    out=bank_i[:, bh, :], lhsT=prodT[i][:, rows], rhs=ident_f[:], is_transpose=True, start=False, stop=True
                )
            if alone:
                nc.vector.tensor_copy(out=st[2, i // 2][:, :, cols], in_=bank_i[:])
            else:
                nc.scalar.copy(out=st[2, i // 2][:, :, cols], in_=bank_i[:])
            if i == LAST:
                nc.scalar.dma_start(out=out_views[2][:, :, i * P : (i + 1) * P], in_=st[2, i // 2][:])
            else:
                store(i, 2)

        for c in range(4):
            for s in (M, Z):
                widen(0, s * H + c * 512, s * H + (c + 1) * 512, c * 512)
        turn_hh(0, M)
        turn_hh(0, Z)
        widen(1, 0, 2 * H, 0)
        widen(2, H, 2 * H, 0)

        gx = const.tile([P, GX * B * 4], BF16, name="gx", align_bytes=64)
        gxw = gx[:].bitcast(F32).rearrange("p (g b u) -> p g b u", g=GX, u=2)
        for bt in range(2):
            turn(x_sb[:, bt, :].bitcast(F32), 0, gxw[:, :, bt * P : (bt + 1) * P, :])
        ga = const.tile([P, GH * B * 4], BF16, name="ga", align_bytes=64)
        gaw = ga[:].bitcast(F32).rearrange("p (g b u) -> p g b u", g=GH, u=2)
        for bt in range(2):
            for g0 in (0, 2):
                turn(h_sb[:, bt, :].bitcast(F32), g0, gaw[:, g0 : g0 + 2, bt * P : (bt + 1) * P, :])
        xq = const.tile([P, GX * B], U32, name="xq", align_bytes=64)
        xs = const.tile([P, GX * B], U8, name="xs", align_bytes=64)
        nc.vector.quantize_mx(out=xq[:].bitcast(FP8X4), scales=xs[:], in_=gx[:])
        hq = const.tile([P, GH * B], U32, name="hq", align_bytes=64)
        hs = const.tile([P, GH * B], U8, name="hs", align_bytes=64)
        nc.vector.quantize_mx(out=hq[:].bitcast(FP8X4), scales=hs[:], in_=ga[:])

        turn_ih(0)
        vps = tp.tile([P, 3 * NU], F32, name="vps", tag="tp")
        for a in range(3):
            nc.tensor.matmul(
                out=vps[:, 0 : 2 * NU], lhsT=vrows[:], rhs=ident_b[:, 32 * a : 32 * (a + 1)], start=(a == 0), stop=(a == 2)
            )
        nc.tensor.matmul(out=vps[:, 2 * NU : 3 * NU], lhsT=vrows[:], rhs=ident_b[:, 96:112], start=True, stop=True)
        bias = const.tile([P, 2 * NU], F32, name="bias")
        nc.scalar.copy(out=bias[:], in_=vps[:, 0 : 2 * NU])
        lam15 = const.tile([P, NU], F32, name="lam15")
        nc.scalar.activation(out=lam15[:], in_=vps[:, 2 * NU : 3 * NU], func=ACT.Exp, bias=math.log(M_SCALE))

        turn_hh(1, M)
        turn_hh(1, Z)
        load_whb(4)
        load_wih(4)

        cT = const.tile([P, NU, B], BF16, name="cT")

        def turn_c(jj):
            cps = tp.tile([P, 2, 2, P], BF16, name="cps", tag="tp")
            for j2 in range(2):
                for bh in range(2):
                    j = 2 * jj + j2
                    nc.tensor.transpose(cps[:, j2, bh, :], c_sb[:, bh, j * P : (j + 1) * P], ident_b[:])
            nc.scalar.copy(out=cT[:, 2 * jj : 2 * jj + 2, :], in_=cps[:].rearrange("p j bh b -> p j (bh b)"))

        turn_ih(1)
        for n in range(1, LAST):
            if n == 2:
                turn_hh(n, M)
                widen(n, 0, H, 0)
            elif n > 2:
                widen(n, 0, 2 * H, 0)
                turn_hh(n, M)
            if 1 < n and n + 3 < NU:
                load_whb(n + 3)
                load_wih(n + 3)
            if n == 1:
                turn_c(0)
            quantize_ih(n - 1)
            multiply(n - 1, M, "x")
            multiply(n - 1, Z, "x")
            if n >= 2:
                turn_hh(n, Z)
            quantize_hh(n - 1)
            if n >= 2:
                product(n - 2)
            multiply(n - 1, M, "h")
            tanh_m(n - 1)
            turn_ih(n + 1)
            if n < NU // 2:
                turn_c(n)
            if n >= 2:
                finish(n - 2)
            multiply(n - 1, Z, "h")
            tanh_z(n - 1)

        widen(LAST, H, 2 * H, 0)
        turn_hh(LAST, M)
        quantize_ih(LAST - 1)
        quantize_hh(LAST - 1)
        product(LAST - 2)
        passes(LAST - 1)
        widen(LAST, 0, H // 2, 0)
        turn_hh(LAST, Z, (0,))
        widen(LAST, H // 2, H, H // 2)
        turn_hh(LAST, Z, (2,))
        finish(LAST - 2)
        quantize_ih(LAST)
        quantize_hh(LAST, GH, GH)
        quantize_hh(LAST, 0, 2)
        product(LAST - 1)
        quantize_hh(LAST, 2, 2)
        multiply(LAST, M, "x")
        multiply(LAST, Z, "x")
        multiply(LAST, M, "h")
        tanh_m(LAST)
        product(LAST)
        multiply(LAST, Z, "h")
        tanh_z(LAST)
        finish(LAST - 1)
        finish(LAST)
